import numpy as np
import ml_dtypes


def mxq(x, axis, fmt="e4m3"):
    dtype, down = {"e4m3": (ml_dtypes.float8_e4m3fn, 7), "e5m2": (ml_dtypes.float8_e5m2, 14)}[fmt]
    v = np.moveaxis(np.asarray(x, np.float32).astype(ml_dtypes.bfloat16).astype(np.float64), axis, -1)
    blocks = v.reshape(v.shape[:-1] + (-1, 32))
    amax = np.abs(blocks).max(-1, keepdims=True)
    byte = np.maximum(np.where(amax > 0, np.frexp(amax)[1] - 1 + 127, 0) - down, 1)
    scale = np.exp2(byte - 127.0)
    codes = (blocks / scale).astype(np.float32).astype(dtype).astype(np.float64)
    return np.moveaxis((codes * scale).reshape(v.shape), -1, axis)


WIDE = False


def mx_kscale(k):
    if not WIDE:
        return np.ones(k)
    levels = np.array([10, -10, 5, -5, 0])
    if k % 512:
        return np.exp2(np.random.permutation(np.resize(levels, k // 32))).repeat(32)
    a = np.empty((k // 512, 16))
    for p in range(k // 512):
        a[p, :8] = np.random.permutation(np.resize(levels, 8))
        for g in range(8):
            far = levels[np.abs(levels - a[p, g]) >= 10]
            a[p, g + 8] = far[np.random.randint(len(far))]
    return np.exp2(a.ravel()).repeat(32)


BF16 = ml_dtypes.bfloat16


def bf(x):
    return np.asarray(x, np.float32).astype(BF16)


def f64(x):
    return np.asarray(x).astype(np.float64)


NM, B, IN, H1, H2, OUT = 8, 128, 512, 512, 512, 128
LS_LO, LS_HI = -20.0, 4.0
MIN_LS, MAX_LS = -20.0, 2.0


def fnoise(ei, ej):
    return np.sign(ei) * np.sign(ej) * np.sqrt(np.abs(ei)) * np.sqrt(np.abs(ej))


def plin(xq, w, b):
    y = xq.transpose(1, 0, 2) @ mxq(f64(w), 2, 'e4m3').transpose(0, 2, 1)
    return y.transpose(1, 0, 2) + f64(b)[None]


def setup_inputs():
    k = mx_kscale(H1)
    t = mx_kscale(H2)
    return {'x1': bf(np.maximum(np.random.standard_normal((B, NM, H1)) * 3.5, 0.0) * k),
            'ei2': bf(np.random.standard_normal((B, NM, 1))),
            'ej2': bf(np.random.standard_normal((1, NM, H2)) * t * t),
            'w21': bf(np.random.standard_normal((NM, H2, H1)) * 0.4 / np.sqrt(H1) / k * t[:, None]),
            'b21': bf(np.random.standard_normal((NM, H2)) * 0.3 * t),
            'w22': bf(np.random.standard_normal((NM, H2, H1)) * 0.48 / np.sqrt(H1) / k),
            'b22': bf(np.random.standard_normal((NM, H2)) * 0.3),
            'w31': bf(np.random.standard_normal((NM, OUT, H2)) * 0.4 / np.sqrt(H2) / t),
            'b31': bf(np.random.standard_normal((NM, OUT)) * 0.3),
            'w32': bf(np.random.standard_normal((NM, OUT, H2)) * 2.4 / np.sqrt(H2) / t),
            'b32': bf(np.random.standard_normal((NM, OUT)) * 2.0 - 9.0)}


def reference(x1, ei2, ej2, w21, b21, w22, b22, w31, b31, w32, b32):
    x1q = mxq(f64(x1), 2, 'e4m3')
    mu = plin(x1q, w21, b21)
    log_sigma = np.clip(plin(x1q, w22, b22), LS_LO, LS_HI)
    x2 = np.maximum(mu + fnoise(f64(ei2), f64(ej2)) * np.exp(log_sigma), 0.0)
    x2q = mxq(x2, 2, 'e4m3')
    m = plin(x2q, w31, b31)
    log_stdev = np.clip(plin(x2q, w32, b32), MIN_LS, MAX_LS)
    return m, log_stdev

@@ -1,0 +1,360 @@
+from contextlib import ExitStack
+
+import concourse.mybir as mybir
+from concourse.masks import make_identity
+
+F32 = mybir.dt.float32
+BF16 = mybir.dt.bfloat16
+U32 = mybir.dt.uint32
+U8 = mybir.dt.uint8
+FP8X4 = mybir.dt.float8_e4m3fn_x4
+ALU = mybir.AluOpType
+ACT = mybir.ActivationFunctionType
+
+P = 128
+NM = 8
+K = 512
+CHUNKS = 4
+MU, LS = 0, 1
+N_BANKS = 5
+FLOPS = 2 * P * NM * (2 * K * K + 2 * K * P)
+
+
+def tile_skill_net_pb_kernel(
+    tc, x1, ei2, ej2, w21, b21, w22, b22, w31, b31, w32, b32, out_0, out_1
+):
+    nc = tc.nc
+    with ExitStack() as ctx:
+        ctx.enter_context(tc.manual_schedule())
+        keep = ctx.enter_context(tc.tile_pool(name="keep", bufs=1))
+        turn = ctx.enter_context(tc.tile_pool(name="turn", bufs=2))
+        psum = ctx.enter_context(tc.psum_pool(name="psum", bufs=1))
+
+        rows = keep.tile([P, K], BF16, name="rows")
+        ei_sb = keep.tile([P, NM], BF16, name="ei_sb")
+        nc.scalar.dma_start(out=ei_sb[:], in_=ei2.rearrange("b j o -> b (j o)"))
+        nc.scalar.dma_start(out=rows[0:8, :], in_=ej2.rearrange("o j h -> (o j) h"))
+        nc.scalar.dma_start(out=rows[8:16, :], in_=b21)
+        nc.scalar.dma_start(out=rows[16:24, :], in_=b22)
+        nc.scalar.dma_start(out=rows[24:32, :], in_=b22)
+        nc.vector.memset(rows[32:64, :], 0.0)
+        nc.vector.memset(rows[64:128, :], 0.0)
+        clip_in = keep.tile([P, 2], F32, name="clip_in")
+        nc.vector.memset(clip_in[:, 0:1], -20.0)
+        nc.vector.memset(clip_in[:, 1:2], 4.0)
+        clip_e = keep.tile([P, 2], F32, name="clip_e")
+        nc.scalar.activation(out=clip_e[:], in_=clip_in[:], func=ACT.Exp)
+        half = keep.tile([P, 8 + CHUNKS * NM], F32, name="half")
+        nc.vector.memset(half[:], 0.5)
+        ident = keep.tile([P, P], F32, name="ident")
+        make_identity(nc, ident[:])
+
+        x1_sb = [keep.tile([P, 4, K], BF16, name="x1_sb%d" % h) for h in range(2)]
+        w2_sb = [[keep.tile([P, CHUNKS, K], BF16, name="w2_sb%d_%d" % (m, j)) for j in range(NM)] for m in range(2)]
+        w3_sb = [[keep.tile([P, 2, K], BF16, name="w3_sb%d_%d" % (m, q)) for q in range(NM // 2)] for m in range(2)]
+        bias3 = keep.tile([P, NM, 2, P], BF16, name="bias3")
+        for h in range(2):
+            nc.sync.dma_start(out=x1_sb[h][:], in_=x1[:, 4 * h : 4 * h + 4, :])
+        for j in range(NM):
+            for m, w in ((LS, w22), (MU, w21)):
+                nc.sync.dma_start(out=w2_sb[m][j][:], in_=w[j].rearrange("(p c) k -> p c k", c=CHUNKS))
+            if j % 2 == 1:
+                q = j // 2
+                for m, w in ((0, w31), (1, w32)):
+                    nc.sync.dma_start(out=w3_sb[m][q][:], in_=w[2 * q : 2 * q + 2].rearrange("j o h -> o j h"))
+        nc.sync.dma_start(out=bias3[:, :, 0, :], in_=b31.partition_broadcast(P))
+        nc.sync.dma_start(out=bias3[:, :, 1, :], in_=b32.partition_broadcast(P))
+
+        banks_used = [0]
+        bank_of = {}
+
+        def next_bank(key):
+            bank_of[key] = psum.tile([P, 4, P], F32, name="bank", tag="bank%d" % (banks_used[0] % N_BANKS))
+            banks_used[0] += 1
+            return bank_of[key]
+
+        def transpose_words(key, sources):
+            bank = next_bank(key)
+            for i, words in enumerate(sources):
+                nc.tensor.transpose(bank[:, i, :], words, ident[:])
+
+        def halves(tile_2d):
+            words = tile_2d.bitcast(F32)
+            return [words[:, 0 : 2 * P : 2], words[:, 1 : 2 * P : 2]]
+
+        def regroup(engine, key, grouped):
+            out = grouped.bitcast(F32).rearrange("p (i c u) -> p i c u", i=2, u=2)
+            in_ = bank_of[key][:].rearrange("p (i u) c -> p i c u", u=2)
+            if engine == "scalar":
+                nc.scalar.copy(out=out, in_=in_)
+            else:
+                nc.vector.tensor_copy(out=out, in_=in_)
+
+        def quantise(grouped, name, pool):
+            width = grouped.shape[1] // 4
+            codes = pool.tile([P, width], U32, name=name + "_c", align_bytes=64)
+            scales = pool.tile([P, width], U8, name=name + "_s", align_bytes=64)
+            nc.vector.quantize_mx(out=codes[:].bitcast(FP8X4), scales=scales[:], in_=grouped)
+            return codes, scales
+
+        def pass_mx(out, stationary, moving, s_cols, m_cols):
+            nc.tensor.matmul_mx(
+                out=out,
+                lhsT=stationary[0][:, s_cols].bitcast(FP8X4),
+                lhsT_scale=stationary[1][:, s_cols],
+                rhs=moving[0][:, m_cols].bitcast(FP8X4),
+                rhs_scale=moving[1][:, m_cols],
+                start=True,
+                stop=True,
+            )
+
+        vec = keep.tile([P, 24 * CHUNKS], BF16, name="vec")
+        draws = keep.tile([P, 8 + CHUNKS * NM], F32, name="draws")
+        bias12 = keep.tile([P, 2, NM, CHUNKS], F32, name="bias12")
+        mag = keep.tile([P, 8 + CHUNKS * NM], F32, name="mag")
+        neg = keep.tile([P, 8 + CHUNKS * NM], F32, name="neg")
+        sgn = keep.tile([P, 8 + CHUNKS * NM], F32, name="sgn")
+        root = keep.tile([P, 8 + CHUNKS * NM], F32, name="root")
+        fac = keep.tile([P, 8 + CHUNKS * NM], F32, name="fac")
+        row_fac = keep.tile([P, NM, P], F32, name="row_fac")
+
+        def noise_factors(cols, pieces):
+            x = draws[:, cols]
+            nc.vector.scalar_tensor_tensor(out=mag[:, cols], in0=x, scalar=-1.0, in1=x, op0=ALU.mult, op1=ALU.max)
+            nc.vector.tensor_single_scalar(out=neg[:, cols], in_=x, scalar=0.0, op=ALU.is_lt)
+            nc.vector.tensor_scalar_max(out=mag[:, cols], in0=mag[:, cols], scalar1=2.0 ** -116)
+            nc.vector.scalar_tensor_tensor(
+                out=sgn[:, cols], in0=x, scalar=0.0, in1=neg[:, cols], op0=ALU.is_gt, op1=ALU.subtract
+            )
+            for piece in pieces:
+                nc.gpsimd.tensor_tensor(out=root[:, piece], in0=mag[:, piece], in1=half[:, piece], op=ALU.pow)
+                nc.gpsimd.tensor_tensor(out=fac[:, piece], in0=root[:, piece], in1=sgn[:, piece], op=ALU.mult)
+
+        def row_draws():
+            nc.vector.tensor_copy(out=draws[:, 0:8], in_=ei_sb[:])
+            noise_factors(slice(0, 8), [slice(0, 8)])
+
+        def hidden_vectors():
+            bank = next_bank("rows")
+            for u, words in enumerate(halves(rows[:])):
+                nc.tensor.transpose(bank[:, u, :], words, ident[:])
+            nc.vector.tensor_copy(
+                out=vec[:].bitcast(F32).rearrange("p (r u) -> p r u", u=2),
+                in_=bank[:, 0:2, 0:24].rearrange("p u r -> p r u"),
+            )
+            nc.vector.tensor_copy(out=draws[:, 8:], in_=vec[:, 0 : CHUNKS * NM])
+            nc.vector.tensor_copy(out=bias12[:].rearrange("p m j c -> p (m j c)"), in_=vec[:, CHUNKS * NM :])
+            noise_factors(
+                slice(8, 8 + CHUNKS * NM), [slice(8 + CHUNKS * j, 8 + CHUNKS * (j + 1)) for j in range(NM)]
+            )
+
+        def spread_row_factor(h):
+            transpose_words(("fi", h), [fac[:, j : j + 1].to_broadcast([P, P]) for j in range(4 * h, 4 * h + 4)])
+
+        def keep_row_factor(h):
+            nc.scalar.copy(out=row_fac[:, 4 * h : 4 * h + 4, :], in_=bank_of[("fi", h)][:])
+
+        x1_g = keep.tile([P, NM * K], BF16, name="x1_g", align_bytes=64)
+        x1_c = keep.tile([P, NM * P], U32, name="x1_c", align_bytes=64)
+        x1_s = keep.tile([P, NM * P], U8, name="x1_s", align_bytes=64)
+
+        def x1_transpose(q):
+            src = x1_sb[q // 2]
+            transpose_words(("x1", q), halves(src[:, 2 * (q % 2), :]) + halves(src[:, 2 * (q % 2) + 1, :]))
+
+        def x1_regroup(q):
+            regroup("scalar", ("x1", q), x1_g[:, 2 * K * q : 2 * K * (q + 1)])
+
+        def x1_quantise(q):
+            nc.vector.quantize_mx(
+                out=x1_c[:, 2 * P * q : 2 * P * (q + 1)].bitcast(FP8X4),
+                scales=x1_s[:, 2 * P * q : 2 * P * (q + 1)],
+                in_=x1_g[:, 2 * K * q : 2 * K * (q + 1)],
+            )
+
+        w2_g = {}
+        w2_q = {}
+
+        def w2_transpose(m, j, hf):
+            src = w2_sb[m][j]
+            transpose_words(("w2", m, j, hf), halves(src[:, 2 * hf, :]) + halves(src[:, 2 * hf + 1, :]))
+
+        def w2_regroup(engine, m, j, hf):
+            if hf == 0:
+                w2_g[(m, j)] = turn.tile([P, CHUNKS * K], BF16, name="w2_g%d" % m, align_bytes=64)
+            regroup(engine, ("w2", m, j, hf), w2_g[(m, j)][:, 2 * K * hf : 2 * K * (hf + 1)])
+
+        def w2_quantise(m, j):
+            w2_q[(m, j)] = quantise(w2_g[(m, j)][:], "w2_%d" % m, turn)
+
+        w3_g = {}
+        w3_q = {}
+
+        def w3_transpose(j):
+            transpose_words(("w3", j), halves(w3_sb[0][j // 2][:, j % 2, :]) + halves(w3_sb[1][j // 2][:, j % 2, :]))
+
+        def w3_regroup(j):
+            w3_g[j] = turn.tile([P, 2 * K], BF16, name="w3_g", align_bytes=64)
+            regroup("scalar", ("w3", j), w3_g[j][:])
+
+        def w3_quantise(j):
+            w3_q[j] = quantise(w3_g[j][:], "w3_%d" % j, keep)
+
+        acc = {}
+        hid = {}
+        x2_q = {}
+
+        def stage1(m, j):
+            tag = "ls" if m == LS else "mu%d" % (j % 2)
+            acc[(m, j)] = psum.tile([P, CHUNKS, P], F32, name="acc", tag=tag)
+            for c in range(CHUNKS):
+                pass_mx(
+                    acc[(m, j)][:, c, :], w2_q[(m, j)], (x1_c, x1_s), slice(P * c, P * (c + 1)), slice(P * j, P * (j + 1))
+                )
+
+        def sigma_exp(j):
+            hid[("e", j)] = turn.tile([P, CHUNKS, P], F32, name="e")
+            for c in range(CHUNKS):
+                nc.scalar.activation(
+                    out=hid[("e", j)][:, c, :],
+                    in_=acc[(LS, j)][:, c, :],
+                    func=ACT.Exp,
+                    bias=bias12[:, LS, j, c : c + 1],
+                    scale=1.0,
+                )
+
+        def sigma_clip(j):
+            hid[("sigma", j)] = turn.tile([P, CHUNKS, P], F32, name="sigma")
+            nc.vector.tensor_scalar(
+                out=hid[("sigma", j)][:],
+                in0=hid[("e", j)][:],
+                scalar1=clip_e[:, 0:1],
+                scalar2=clip_e[:, 1:2],
+                op0=ALU.max,
+                op1=ALU.min,
+            )
+
+        def noise_and_sum(j):
+            noisy = turn.tile([P, CHUNKS, P], F32, name="noisy")
+            hid[("sum", j)] = turn.tile([P, CHUNKS, P], F32, name="total")
+            for c in range(CHUNKS):
+                nc.vector.scalar_tensor_tensor(
+                    out=noisy[:, c, :],
+                    in0=hid[("sigma", j)][:, c, :],
+                    scalar=fac[:, 8 + CHUNKS * j + c : 9 + CHUNKS * j + c],
+                    in1=row_fac[:, j, :],
+                    op0=ALU.mult,
+                    op1=ALU.mult,
+                )
+            for c in range(CHUNKS):
+                nc.vector.scalar_tensor_tensor(
+                    out=hid[("sum", j)][:, c, :],
+                    in0=acc[(MU, j)][:, c, :],
+                    scalar=bias12[:, MU, j, c : c + 1],
+                    in1=noisy[:, c, :],
+                    op0=ALU.add,
+                    op1=ALU.add,
+                )
+
+        def relu_regroup(j):
+            hid[("x2", j)] = turn.tile([P, K], BF16, name="x2_g", align_bytes=64)
+            nc.scalar.activation(
+                out=hid[("x2", j)][:].rearrange("p (b c) -> p b c", c=CHUNKS),
+                in_=hid[("sum", j)][:].rearrange("p c b -> p b c"),
+                func=ACT.Relu,
+            )
+
+        def x2_quantise(j):
+            x2_q[j] = quantise(hid[("x2", j)][:], "x2_%d" % j, keep)
+
+        def stage2(q):
+            bank = next_bank(("heads", q))
+            for i in range(2):
+                j = 2 * q + i
+                pass_mx(
+                    bank[:, 2 * i : 2 * i + 2, :].rearrange("p m o -> p (m o)"),
+                    x2_q[j],
+                    w3_q[j],
+                    slice(0, P),
+                    slice(0, 2 * P),
+                )
+
+        def heads_out(q):
+            sums = bank_of[("heads", q)][:].rearrange("p (i m) o -> p i m o", m=2)
+            res = keep.tile([P, 2, 2, P], F32, name="res%d" % q)
+            pair = slice(2 * q, 2 * q + 2)
+            for m in (1, 0):
+                nc.vector.tensor_tensor(out=res[:, :, m, :], in0=sums[:, :, m, :], in1=bias3[:, pair, m, :], op=ALU.add)
+            nc.sync.dma_start(out=out_0[:, pair, :], in_=res[:, :, 0, :])
+            nc.vector.tensor_scalar(
+                out=res[:, :, 1, :], in0=res[:, :, 1, :], scalar1=-20.0, scalar2=2.0, op0=ALU.max, op1=ALU.min
+            )
+            nc.sync.dma_start(out=out_1[:, pair, :], in_=res[:, :, 1, :])
+
+        def live(j):
+            return 0 <= j < NM
+
+        row_draws()
+        for q in (0, 1):
+            x1_transpose(q)
+            x1_regroup(q)
+        hidden_vectors()
+        for q in (2, 3):
+            x1_transpose(q)
+            x1_regroup(q)
+        x1_quantise(0)
+        x1_quantise(1)
+
+        for j in range(-2, NM):
+            if live(j + 1):
+                w2_regroup("scalar", MU, j + 1, 0)
+                w2_regroup("scalar", MU, j + 1, 1)
+            if live(j):
+                w3_transpose(j)
+            if live(j + 2):
+                w2_transpose(LS, j + 2, 0)
+                w2_transpose(LS, j + 2, 1)
+            if live(j):
+                sigma_clip(j)
+            if live(j + 1):
+                w2_quantise(LS, j + 1)
+            if live(j):
+                noise_and_sum(j)
+                w3_regroup(j)
+            if live(j + 2):
+                w2_regroup("scalar", LS, j + 2, 0)
+            if live(j + 1):
+                stage1(LS, j + 1)
+            if j == -1:
+                spread_row_factor(0)
+                spread_row_factor(1)
+            if live(j + 2):
+                w2_transpose(MU, j + 2, 0)
+                w2_transpose(MU, j + 2, 1)
+            if live(j + 1):
+                w2_quantise(MU, j + 1)
+            if live(j - 1):
+                x2_quantise(j - 1)
+            if live(j + 2):
+                w2_regroup("vector", LS, j + 2, 1)
+            if j == -1:
+                x1_quantise(2)
+                x1_quantise(3)
+            if live(j + 1):
+                sigma_exp(j + 1)
+            if j == -1:
+                keep_row_factor(0)
+                keep_row_factor(1)
+            if live(j):
+                relu_regroup(j)
+                w3_quantise(j)
+            if live(j + 1):
+                stage1(MU, j + 1)
+
+        for q in range(NM // 2 - 1):
+            stage2(q)
+        heads_out(0)
+        x2_quantise(NM - 1)
+        stage2(NM // 2 - 1)
+        for q in range(1, NM // 2):
+            heads_out(q)

@@ -32,20 +32,19 @@ def tile_skill_net_pb_kernel(
 
         rows = keep.tile([P, K], BF16, name="rows")
         ei_sb = keep.tile([P, NM], BF16, name="ei_sb")
-        nc.scalar.dma_start(out=ei_sb[:], in_=ei2.rearrange("b j o -> b (j o)"))
-        nc.scalar.dma_start(out=rows[0:8, :], in_=ej2.rearrange("o j h -> (o j) h"))
-        nc.scalar.dma_start(out=rows[8:16, :], in_=b21)
-        nc.scalar.dma_start(out=rows[16:24, :], in_=b22)
-        nc.scalar.dma_start(out=rows[24:32, :], in_=b22)
+        nc.sync.dma_start(out=rows[0:8, :], in_=ej2.rearrange("o j h -> (o j) h"))
+        nc.sync.dma_start(out=ei_sb[:], in_=ei2.rearrange("b j o -> b (j o)"))
+        nc.sync.dma_start(out=rows[8:16, :], in_=b21)
+        nc.sync.dma_start(out=rows[16:24, :], in_=b22)
+        nc.sync.dma_start(out=rows[24:32, :], in_=b22)
         nc.vector.memset(rows[32:64, :], 0.0)
         nc.vector.memset(rows[64:128, :], 0.0)
         clip_in = keep.tile([P, 2], F32, name="clip_in")
         nc.vector.memset(clip_in[:, 0:1], -20.0)
         nc.vector.memset(clip_in[:, 1:2], 4.0)
         clip_e = keep.tile([P, 2], F32, name="clip_e")
-        nc.scalar.activation(out=clip_e[:], in_=clip_in[:], func=ACT.Exp)
-        half = keep.tile([P, 8 + CHUNKS * NM], F32, name="half")
-        nc.vector.memset(half[:], 0.5)
+        warm = keep.tile([P, 1], F32, name="warm")
+        nc.scalar.activation(out=warm[:], in_=clip_in[:, 1:2], func=ACT.Sqrt)
         ident = keep.tile([P, P], F32, name="ident")
         make_identity(nc, ident[:])
 
@@ -118,35 +117,32 @@ def tile_skill_net_pb_kernel(
         fac = keep.tile([P, 8 + CHUNKS * NM], F32, name="fac")
         row_fac = keep.tile([P, NM, P], F32, name="row_fac")
 
-        def noise_factors(cols, pieces):
+        def magnitude_and_sign(cols):
             x = draws[:, cols]
             nc.vector.scalar_tensor_tensor(out=mag[:, cols], in0=x, scalar=-1.0, in1=x, op0=ALU.mult, op1=ALU.max)
             nc.vector.tensor_single_scalar(out=neg[:, cols], in_=x, scalar=0.0, op=ALU.is_lt)
-            nc.vector.tensor_scalar_max(out=mag[:, cols], in0=mag[:, cols], scalar1=2.0 ** -116)
             nc.vector.scalar_tensor_tensor(
                 out=sgn[:, cols], in0=x, scalar=0.0, in1=neg[:, cols], op0=ALU.is_gt, op1=ALU.subtract
             )
-            for piece in pieces:
-                nc.gpsimd.tensor_tensor(out=root[:, piece], in0=mag[:, piece], in1=half[:, piece], op=ALU.pow)
-                nc.gpsimd.tensor_tensor(out=fac[:, piece], in0=root[:, piece], in1=sgn[:, piece], op=ALU.mult)
 
-        def row_draws():
-            nc.vector.tensor_copy(out=draws[:, 0:8], in_=ei_sb[:])
-            noise_factors(slice(0, 8), [slice(0, 8)])
+        def noise_factors(cols):
+            nc.scalar.activation(out=root[:, cols], in_=mag[:, cols], func=ACT.Sqrt)
+            nc.vector.tensor_tensor(out=fac[:, cols], in0=root[:, cols], in1=sgn[:, cols], op=ALU.mult)
 
-        def hidden_vectors():
+        def small_vectors():
             bank = next_bank("rows")
             for u, words in enumerate(halves(rows[:])):
                 nc.tensor.transpose(bank[:, u, :], words, ident[:])
+            nc.vector.tensor_copy(out=draws[:, 0:8], in_=ei_sb[:])
             nc.vector.tensor_copy(
                 out=vec[:].bitcast(F32).rearrange("p (r u) -> p r u", u=2),
                 in_=bank[:, 0:2, 0:24].rearrange("p u r -> p r u"),
             )
             nc.vector.tensor_copy(out=draws[:, 8:], in_=vec[:, 0 : CHUNKS * NM])
             nc.vector.tensor_copy(out=bias12[:].rearrange("p m j c -> p (m j c)"), in_=vec[:, CHUNKS * NM :])
-            noise_factors(
-                slice(8, 8 + CHUNKS * NM), [slice(8 + CHUNKS * j, 8 + CHUNKS * (j + 1)) for j in range(NM)]
-            )
+            magnitude_and_sign(slice(0, 8 + CHUNKS * NM))
+            noise_factors(slice(0, 8 + CHUNKS * NM))
+            nc.scalar.activation(out=clip_e[:], in_=clip_in[:], func=ACT.Exp)
 
         def spread_row_factor(h):
             transpose_words(("fi", h), [fac[:, j : j + 1].to_broadcast([P, P]) for j in range(4 * h, 4 * h + 4)])
@@ -163,7 +159,7 @@ def tile_skill_net_pb_kernel(
             transpose_words(("x1", q), halves(src[:, 2 * (q % 2), :]) + halves(src[:, 2 * (q % 2) + 1, :]))
 
         def x1_regroup(q):
-            regroup("scalar", ("x1", q), x1_g[:, 2 * K * q : 2 * K * (q + 1)])
+            regroup("vector" if q < 2 else "scalar", ("x1", q), x1_g[:, 2 * K * q : 2 * K * (q + 1)])
 
         def x1_quantise(q):
             nc.vector.quantize_mx(
@@ -294,12 +290,8 @@ def tile_skill_net_pb_kernel(
         def live(j):
             return 0 <= j < NM
 
-        row_draws()
-        for q in (0, 1):
-            x1_transpose(q)
-            x1_regroup(q)
-        hidden_vectors()
-        for q in (2, 3):
+        small_vectors()
+        for q in range(NM // 2):
             x1_transpose(q)
             x1_regroup(q)
         x1_quantise(0)

@@ -16,7 +16,10 @@ NM = 8
 K = 512
 CHUNKS = 4
 MU, LS = 0, 1
-N_BANKS = 5
+RELU_ON_SCALAR_FROM = 6
+BIAS_AFTER = 5
+EARLY_HEADS = {3: 0}
+N_BANKS = 4
 FLOPS = 2 * P * NM * (2 * K * K + 2 * K * P)
 
 
@@ -61,8 +64,9 @@ def tile_skill_net_pb_kernel(
                 q = j // 2
                 for m, w in ((0, w31), (1, w32)):
                     nc.sync.dma_start(out=w3_sb[m][q][:], in_=w[2 * q : 2 * q + 2].rearrange("j o h -> o j h"))
-        nc.sync.dma_start(out=bias3[:, :, 0, :], in_=b31.partition_broadcast(P))
-        nc.sync.dma_start(out=bias3[:, :, 1, :], in_=b32.partition_broadcast(P))
+            if j == BIAS_AFTER:
+                nc.sync.dma_start(out=bias3[:, :, 0, :], in_=b31.partition_broadcast(P))
+                nc.sync.dma_start(out=bias3[:, :, 1, :], in_=b32.partition_broadcast(P))
 
         banks_used = [0]
         bank_of = {}
@@ -115,7 +119,7 @@ def tile_skill_net_pb_kernel(
         sgn = keep.tile([P, 8 + CHUNKS * NM], F32, name="sgn")
         root = keep.tile([P, 8 + CHUNKS * NM], F32, name="root")
         fac = keep.tile([P, 8 + CHUNKS * NM], F32, name="fac")
-        row_fac = keep.tile([P, NM, P], F32, name="row_fac")
+        row_fac = [psum.tile([P, 4, P], F32, name="row_fac%d" % h) for h in range(2)]
 
         def magnitude_and_sign(cols):
             x = draws[:, cols]
@@ -145,10 +149,8 @@ def tile_skill_net_pb_kernel(
             nc.scalar.activation(out=clip_e[:], in_=clip_in[:], func=ACT.Exp)
 
         def spread_row_factor(h):
-            transpose_words(("fi", h), [fac[:, j : j + 1].to_broadcast([P, P]) for j in range(4 * h, 4 * h + 4)])
-
-        def keep_row_factor(h):
-            nc.scalar.copy(out=row_fac[:, 4 * h : 4 * h + 4, :], in_=bank_of[("fi", h)][:])
+            for i in range(4):
+                nc.tensor.transpose(row_fac[h][:, i, :], fac[:, 4 * h + i : 4 * h + i + 1].to_broadcast([P, P]), ident[:])
 
         x1_g = keep.tile([P, NM * K], BF16, name="x1_g", align_bytes=64)
         x1_c = keep.tile([P, NM * P], U32, name="x1_c", align_bytes=64)
@@ -201,7 +203,7 @@ def tile_skill_net_pb_kernel(
         x2_q = {}
 
         def stage1(m, j):
-            tag = "ls" if m == LS else "mu%d" % (j % 2)
+            tag = "ls" if m == LS else "mu"
             acc[(m, j)] = psum.tile([P, CHUNKS, P], F32, name="acc", tag=tag)
             for c in range(CHUNKS):
                 pass_mx(
@@ -238,7 +240,7 @@ def tile_skill_net_pb_kernel(
                     out=noisy[:, c, :],
                     in0=hid[("sigma", j)][:, c, :],
                     scalar=fac[:, 8 + CHUNKS * j + c : 9 + CHUNKS * j + c],
-                    in1=row_fac[:, j, :],
+                    in1=row_fac[j // 4][:, j % 4, :],
                     op0=ALU.mult,
                     op1=ALU.mult,
                 )
@@ -254,11 +256,18 @@ def tile_skill_net_pb_kernel(
 
         def relu_regroup(j):
             hid[("x2", j)] = turn.tile([P, K], BF16, name="x2_g", align_bytes=64)
-            nc.scalar.activation(
-                out=hid[("x2", j)][:].rearrange("p (b c) -> p b c", c=CHUNKS),
-                in_=hid[("sum", j)][:].rearrange("p c b -> p b c"),
-                func=ACT.Relu,
-            )
+            if j < RELU_ON_SCALAR_FROM:
+                nc.vector.tensor_scalar_max(
+                    out=hid[("x2", j)][:].rearrange("p (b c) -> p b c", c=CHUNKS),
+                    in0=hid[("sum", j)][:].rearrange("p c b -> p b c"),
+                    scalar1=0.0,
+                )
+            else:
+                nc.scalar.activation(
+                    out=hid[("x2", j)][:].rearrange("p (b c) -> p b c", c=CHUNKS),
+                    in_=hid[("sum", j)][:].rearrange("p c b -> p b c"),
+                    func=ACT.Relu,
+                )
 
         def x2_quantise(j):
             x2_q[j] = quantise(hid[("x2", j)][:], "x2_%d" % j, keep)
@@ -308,6 +317,8 @@ def tile_skill_net_pb_kernel(
                 w2_transpose(LS, j + 2, 1)
             if live(j):
                 sigma_clip(j)
+            if j == NM - 1:
+                w3_quantise(j - 1)
             if live(j + 1):
                 w2_quantise(LS, j + 1)
             if live(j):
@@ -317,6 +328,8 @@ def tile_skill_net_pb_kernel(
                 w2_regroup("scalar", LS, j + 2, 0)
             if live(j + 1):
                 stage1(LS, j + 1)
+            if j in EARLY_HEADS:
+                stage2(EARLY_HEADS[j])
             if j == -1:
                 spread_row_factor(0)
                 spread_row_factor(1)
@@ -325,28 +338,33 @@ def tile_skill_net_pb_kernel(
                 w2_transpose(MU, j + 2, 1)
             if live(j + 1):
                 w2_quantise(MU, j + 1)
-            if live(j - 1):
-                x2_quantise(j - 1)
+            if live(j) and j < RELU_ON_SCALAR_FROM:
+                relu_regroup(j)
             if live(j + 2):
-                w2_regroup("vector", LS, j + 2, 1)
+                w2_regroup("vector" if j < 0 else "scalar", LS, j + 2, 1)
             if j == -1:
                 x1_quantise(2)
                 x1_quantise(3)
             if live(j + 1):
                 sigma_exp(j + 1)
-            if j == -1:
-                keep_row_factor(0)
-                keep_row_factor(1)
-            if live(j):
+            if live(j) and j >= RELU_ON_SCALAR_FROM:
                 relu_regroup(j)
+            if live(j) and j < NM - 2:
                 w3_quantise(j)
+                x2_quantise(j)
+            if j in EARLY_HEADS:
+                heads_out(EARLY_HEADS[j])
             if live(j + 1):
                 stage1(MU, j + 1)
 
-        for q in range(NM // 2 - 1):
+        late = [q for q in range(NM // 2) if q not in EARLY_HEADS.values()]
+        for q in late[:-1]:
             stage2(q)
-        heads_out(0)
+        x2_quantise(NM - 2)
+        w3_quantise(NM - 1)
+        for q in late[:1]:
+            heads_out(q)
         x2_quantise(NM - 1)
-        stage2(NM // 2 - 1)
-        for q in range(1, NM // 2):
+        stage2(late[-1])
+        for q in late[1:]:
             heads_out(q)

@@ -19,7 +19,7 @@ MU, LS = 0, 1
 RELU_ON_SCALAR_FROM = 6
 BIAS_AFTER = 5
 EARLY_HEADS = {3: 0}
-N_BANKS = 4
+N_BANKS = 5
 FLOPS = 2 * P * NM * (2 * K * K + 2 * K * P)
 
 
@@ -119,7 +119,7 @@ def tile_skill_net_pb_kernel(
         sgn = keep.tile([P, 8 + CHUNKS * NM], F32, name="sgn")
         root = keep.tile([P, 8 + CHUNKS * NM], F32, name="root")
         fac = keep.tile([P, 8 + CHUNKS * NM], F32, name="fac")
-        row_fac = [psum.tile([P, 4, P], F32, name="row_fac%d" % h) for h in range(2)]
+        row_fac = keep.tile([P, NM, P], F32, name="row_fac")
 
         def magnitude_and_sign(cols):
             x = draws[:, cols]
@@ -149,8 +149,10 @@ def tile_skill_net_pb_kernel(
             nc.scalar.activation(out=clip_e[:], in_=clip_in[:], func=ACT.Exp)
 
         def spread_row_factor(h):
-            for i in range(4):
-                nc.tensor.transpose(row_fac[h][:, i, :], fac[:, 4 * h + i : 4 * h + i + 1].to_broadcast([P, P]), ident[:])
+            transpose_words(("fi", h), [fac[:, j : j + 1].to_broadcast([P, P]) for j in range(4 * h, 4 * h + 4)])
+
+        def keep_row_factor(h):
+            nc.scalar.copy(out=row_fac[:, 4 * h : 4 * h + 4, :], in_=bank_of[("fi", h)][:])
 
         x1_g = keep.tile([P, NM * K], BF16, name="x1_g", align_bytes=64)
         x1_c = keep.tile([P, NM * P], U32, name="x1_c", align_bytes=64)
@@ -203,7 +205,7 @@ def tile_skill_net_pb_kernel(
         x2_q = {}
 
         def stage1(m, j):
-            tag = "ls" if m == LS else "mu"
+            tag = "ls" if m == LS else "mu%d" % (j % 2)
             acc[(m, j)] = psum.tile([P, CHUNKS, P], F32, name="acc", tag=tag)
             for c in range(CHUNKS):
                 pass_mx(
@@ -240,7 +242,7 @@ def tile_skill_net_pb_kernel(
                     out=noisy[:, c, :],
                     in0=hid[("sigma", j)][:, c, :],
                     scalar=fac[:, 8 + CHUNKS * j + c : 9 + CHUNKS * j + c],
-                    in1=row_fac[j // 4][:, j % 4, :],
+                    in1=row_fac[:, j, :],
                     op0=ALU.mult,
                     op1=ALU.mult,
                 )
@@ -347,6 +349,9 @@ def tile_skill_net_pb_kernel(
                 x1_quantise(3)
             if live(j + 1):
                 sigma_exp(j + 1)
+            if j == -1:
+                keep_row_factor(0)
+                keep_row_factor(1)
             if live(j) and j >= RELU_ON_SCALAR_FROM:
                 relu_regroup(j)
             if live(j) and j < NM - 2:

@@ -51,12 +51,12 @@ def tile_skill_net_pb_kernel(
         ident = keep.tile([P, P], F32, name="ident")
         make_identity(nc, ident[:])
 
-        x1_sb = [keep.tile([P, 4, K], BF16, name="x1_sb%d" % h) for h in range(2)]
+        x1_sb = [keep.tile([P, 2, K], BF16, name="x1_sb%d" % q) for q in range(NM // 2)]
         w2_sb = [[keep.tile([P, CHUNKS, K], BF16, name="w2_sb%d_%d" % (m, j)) for j in range(NM)] for m in range(2)]
         w3_sb = [[keep.tile([P, 2, K], BF16, name="w3_sb%d_%d" % (m, q)) for q in range(NM // 2)] for m in range(2)]
         bias3 = keep.tile([P, NM, 2, P], BF16, name="bias3")
-        for h in range(2):
-            nc.sync.dma_start(out=x1_sb[h][:], in_=x1[:, 4 * h : 4 * h + 4, :])
+        for q in range(NM // 2):
+            nc.sync.dma_start(out=x1_sb[q][:], in_=x1[:, 2 * q : 2 * q + 2, :])
         for j in range(NM):
             for m, w in ((LS, w22), (MU, w21)):
                 nc.sync.dma_start(out=w2_sb[m][j][:], in_=w[j].rearrange("(p c) k -> p c k", c=CHUNKS))
@@ -152,15 +152,14 @@ def tile_skill_net_pb_kernel(
             transpose_words(("fi", h), [fac[:, j : j + 1].to_broadcast([P, P]) for j in range(4 * h, 4 * h + 4)])
 
         def keep_row_factor(h):
-            nc.scalar.copy(out=row_fac[:, 4 * h : 4 * h + 4, :], in_=bank_of[("fi", h)][:])
+            nc.vector.tensor_copy(out=row_fac[:, 4 * h : 4 * h + 4, :], in_=bank_of[("fi", h)][:])
 
         x1_g = keep.tile([P, NM * K], BF16, name="x1_g", align_bytes=64)
         x1_c = keep.tile([P, NM * P], U32, name="x1_c", align_bytes=64)
         x1_s = keep.tile([P, NM * P], U8, name="x1_s", align_bytes=64)
 
         def x1_transpose(q):
-            src = x1_sb[q // 2]
-            transpose_words(("x1", q), halves(src[:, 2 * (q % 2), :]) + halves(src[:, 2 * (q % 2) + 1, :]))
+            transpose_words(("x1", q), halves(x1_sb[q][:, 0, :]) + halves(x1_sb[q][:, 1, :]))
 
         def x1_regroup(q):
             regroup("vector" if q < 2 else "scalar", ("x1", q), x1_g[:, 2 * K * q : 2 * K * (q + 1)])
@@ -307,6 +306,9 @@ def tile_skill_net_pb_kernel(
             x1_regroup(q)
         x1_quantise(0)
         x1_quantise(1)
+        for h in range(2):
+            spread_row_factor(h)
+            keep_row_factor(h)
 
         for j in range(-2, NM):
             if live(j + 1):
@@ -332,9 +334,6 @@ def tile_skill_net_pb_kernel(
                 stage1(LS, j + 1)
             if j in EARLY_HEADS:
                 stage2(EARLY_HEADS[j])
-            if j == -1:
-                spread_row_factor(0)
-                spread_row_factor(1)
             if live(j + 2):
                 w2_transpose(MU, j + 2, 0)
                 w2_transpose(MU, j + 2, 1)
@@ -349,9 +348,6 @@ def tile_skill_net_pb_kernel(
                 x1_quantise(3)
             if live(j + 1):
                 sigma_exp(j + 1)
-            if j == -1:
-                keep_row_factor(0)
-                keep_row_factor(1)
             if live(j) and j >= RELU_ON_SCALAR_FROM:
                 relu_regroup(j)
             if live(j) and j < NM - 2:

@@ -17,8 +17,8 @@ K = 512
 CHUNKS = 4
 MU, LS = 0, 1
 RELU_ON_SCALAR_FROM = 6
-BIAS_AFTER = 5
-EARLY_HEADS = {3: 0}
+BIAS_AFTER = 7
+EARLY_HEADS = {}
 N_BANKS = 5
 FLOPS = 2 * P * NM * (2 * K * K + 2 * K * P)
 

@@ -259,8 +259,8 @@ def tile_skill_net_pb_kernel(
             hid[("x2", j)] = turn.tile([P, K], BF16, name="x2_g", align_bytes=64)
             if j < RELU_ON_SCALAR_FROM:
                 nc.vector.tensor_scalar_max(
-                    out=hid[("x2", j)][:].rearrange("p (b c) -> p b c", c=CHUNKS),
-                    in0=hid[("sum", j)][:].rearrange("p c b -> p b c"),
+                    out=hid[("x2", j)][:].rearrange("p (g i c) -> p g c i", i=4, c=CHUNKS),
+                    in0=hid[("sum", j)][:].rearrange("p c (g i) -> p g c i", i=4),
                     scalar1=0.0,
                 )
             else:

from contextlib import ExitStack

import concourse.mybir as mybir
from concourse.masks import make_identity

F32 = mybir.dt.float32
BF16 = mybir.dt.bfloat16
U32 = mybir.dt.uint32
U8 = mybir.dt.uint8
FP8X4 = mybir.dt.float8_e4m3fn_x4
ALU = mybir.AluOpType
ACT = mybir.ActivationFunctionType

P = 128
NM = 8
K = 512
CHUNKS = 4
MU, LS = 0, 1
RELU_ON_SCALAR_FROM = 6
BIAS_AFTER = 7
EARLY_HEADS = {}
N_BANKS = 5
FLOPS = 2 * P * NM * (2 * K * K + 2 * K * P)


def tile_skill_net_pb_kernel(
    tc, x1, ei2, ej2, w21, b21, w22, b22, w31, b31, w32, b32, out_0, out_1
):
    nc = tc.nc
    with ExitStack() as ctx:
        ctx.enter_context(tc.manual_schedule())
        keep = ctx.enter_context(tc.tile_pool(name="keep", bufs=1))
        turn = ctx.enter_context(tc.tile_pool(name="turn", bufs=2))
        psum = ctx.enter_context(tc.psum_pool(name="psum", bufs=1))

        rows = keep.tile([P, K], BF16, name="rows")
        ei_sb = keep.tile([P, NM], BF16, name="ei_sb")
        nc.sync.dma_start(out=rows[0:8, :], in_=ej2.rearrange("o j h -> (o j) h"))
        nc.sync.dma_start(out=ei_sb[:], in_=ei2.rearrange("b j o -> b (j o)"))
        nc.sync.dma_start(out=rows[8:16, :], in_=b21)
        nc.sync.dma_start(out=rows[16:24, :], in_=b22)
        nc.sync.dma_start(out=rows[24:32, :], in_=b22)
        nc.vector.memset(rows[32:64, :], 0.0)
        nc.vector.memset(rows[64:128, :], 0.0)
        clip_in = keep.tile([P, 2], F32, name="clip_in")
        nc.vector.memset(clip_in[:, 0:1], -20.0)
        nc.vector.memset(clip_in[:, 1:2], 4.0)
        clip_e = keep.tile([P, 2], F32, name="clip_e")
        warm = keep.tile([P, 1], F32, name="warm")
        nc.scalar.activation(out=warm[:], in_=clip_in[:, 1:2], func=ACT.Sqrt)
        ident = keep.tile([P, P], F32, name="ident")
        make_identity(nc, ident[:])

        x1_sb = [keep.tile([P, 2, K], BF16, name="x1_sb%d" % q) for q in range(NM // 2)]
        w2_sb = [[keep.tile([P, CHUNKS, K], BF16, name="w2_sb%d_%d" % (m, j)) for j in range(NM)] for m in range(2)]
        w3_sb = [[keep.tile([P, 2, K], BF16, name="w3_sb%d_%d" % (m, q)) for q in range(NM // 2)] for m in range(2)]
        bias3 = keep.tile([P, NM, 2, P], BF16, name="bias3")
        for q in range(NM // 2):
            nc.sync.dma_start(out=x1_sb[q][:], in_=x1[:, 2 * q : 2 * q + 2, :])
        for j in range(NM):
            for m, w in ((LS, w22), (MU, w21)):
                nc.sync.dma_start(out=w2_sb[m][j][:], in_=w[j].rearrange("(p c) k -> p c k", c=CHUNKS))
            if j % 2 == 1:
                q = j // 2
                for m, w in ((0, w31), (1, w32)):
                    nc.sync.dma_start(out=w3_sb[m][q][:], in_=w[2 * q : 2 * q + 2].rearrange("j o h -> o j h"))
            if j == BIAS_AFTER:
                nc.sync.dma_start(out=bias3[:, :, 0, :], in_=b31.partition_broadcast(P))
                nc.sync.dma_start(out=bias3[:, :, 1, :], in_=b32.partition_broadcast(P))

        banks_used = [0]
        bank_of = {}

        def next_bank(key):
            bank_of[key] = psum.tile([P, 4, P], F32, name="bank", tag="bank%d" % (banks_used[0] % N_BANKS))
            banks_used[0] += 1
            return bank_of[key]

        def transpose_words(key, sources):
            bank = next_bank(key)
            for i, words in enumerate(sources):
                nc.tensor.transpose(bank[:, i, :], words, ident[:])

        def halves(tile_2d):
            words = tile_2d.bitcast(F32)
            return [words[:, 0 : 2 * P : 2], words[:, 1 : 2 * P : 2]]

        def regroup(engine, key, grouped):
            out = grouped.bitcast(F32).rearrange("p (i c u) -> p i c u", i=2, u=2)
            in_ = bank_of[key][:].rearrange("p (i u) c -> p i c u", u=2)
            if engine == "scalar":
                nc.scalar.copy(out=out, in_=in_)
            else:
                nc.vector.tensor_copy(out=out, in_=in_)

        def quantise(grouped, name, pool):
            width = grouped.shape[1] // 4
            codes = pool.tile([P, width], U32, name=name + "_c", align_bytes=64)
            scales = pool.tile([P, width], U8, name=name + "_s", align_bytes=64)
            nc.vector.quantize_mx(out=codes[:].bitcast(FP8X4), scales=scales[:], in_=grouped)
            return codes, scales

        def pass_mx(out, stationary, moving, s_cols, m_cols):
            nc.tensor.matmul_mx(
                out=out,
                lhsT=stationary[0][:, s_cols].bitcast(FP8X4),
                lhsT_scale=stationary[1][:, s_cols],
                rhs=moving[0][:, m_cols].bitcast(FP8X4),
                rhs_scale=moving[1][:, m_cols],
                start=True,
                stop=True,
            )

        vec = keep.tile([P, 24 * CHUNKS], BF16, name="vec")
        draws = keep.tile([P, 8 + CHUNKS * NM], F32, name="draws")
        bias12 = keep.tile([P, 2, NM, CHUNKS], F32, name="bias12")
        mag = keep.tile([P, 8 + CHUNKS * NM], F32, name="mag")
        neg = keep.tile([P, 8 + CHUNKS * NM], F32, name="neg")
        sgn = keep.tile([P, 8 + CHUNKS * NM], F32, name="sgn")
        root = keep.tile([P, 8 + CHUNKS * NM], F32, name="root")
        fac = keep.tile([P, 8 + CHUNKS * NM], F32, name="fac")
        row_fac = keep.tile([P, NM, P], F32, name="row_fac")

        def magnitude_and_sign(cols):
            x = draws[:, cols]
            nc.vector.scalar_tensor_tensor(out=mag[:, cols], in0=x, scalar=-1.0, in1=x, op0=ALU.mult, op1=ALU.max)
            nc.vector.tensor_single_scalar(out=neg[:, cols], in_=x, scalar=0.0, op=ALU.is_lt)
            nc.vector.scalar_tensor_tensor(
                out=sgn[:, cols], in0=x, scalar=0.0, in1=neg[:, cols], op0=ALU.is_gt, op1=ALU.subtract
            )

        def noise_factors(cols):
            nc.scalar.activation(out=root[:, cols], in_=mag[:, cols], func=ACT.Sqrt)
            nc.vector.tensor_tensor(out=fac[:, cols], in0=root[:, cols], in1=sgn[:, cols], op=ALU.mult)

        def small_vectors():
            bank = next_bank("rows")
            for u, words in enumerate(halves(rows[:])):
                nc.tensor.transpose(bank[:, u, :], words, ident[:])
            nc.vector.tensor_copy(out=draws[:, 0:8], in_=ei_sb[:])
            nc.vector.tensor_copy(
                out=vec[:].bitcast(F32).rearrange("p (r u) -> p r u", u=2),
                in_=bank[:, 0:2, 0:24].rearrange("p u r -> p r u"),
            )
            nc.vector.tensor_copy(out=draws[:, 8:], in_=vec[:, 0 : CHUNKS * NM])
            nc.vector.tensor_copy(out=bias12[:].rearrange("p m j c -> p (m j c)"), in_=vec[:, CHUNKS * NM :])
            magnitude_and_sign(slice(0, 8 + CHUNKS * NM))
            noise_factors(slice(0, 8 + CHUNKS * NM))
            nc.scalar.activation(out=clip_e[:], in_=clip_in[:], func=ACT.Exp)

        def spread_row_factor(h):
            transpose_words(("fi", h), [fac[:, j : j + 1].to_broadcast([P, P]) for j in range(4 * h, 4 * h + 4)])

        def keep_row_factor(h):
            nc.vector.tensor_copy(out=row_fac[:, 4 * h : 4 * h + 4, :], in_=bank_of[("fi", h)][:])

        x1_g = keep.tile([P, NM * K], BF16, name="x1_g", align_bytes=64)
        x1_c = keep.tile([P, NM * P], U32, name="x1_c", align_bytes=64)
        x1_s = keep.tile([P, NM * P], U8, name="x1_s", align_bytes=64)

        def x1_transpose(q):
            transpose_words(("x1", q), halves(x1_sb[q][:, 0, :]) + halves(x1_sb[q][:, 1, :]))

        def x1_regroup(q):
            regroup("vector" if q < 2 else "scalar", ("x1", q), x1_g[:, 2 * K * q : 2 * K * (q + 1)])

        def x1_quantise(q):
            nc.vector.quantize_mx(
                out=x1_c[:, 2 * P * q : 2 * P * (q + 1)].bitcast(FP8X4),
                scales=x1_s[:, 2 * P * q : 2 * P * (q + 1)],
                in_=x1_g[:, 2 * K * q : 2 * K * (q + 1)],
            )

        w2_g = {}
        w2_q = {}

        def w2_transpose(m, j, hf):
            src = w2_sb[m][j]
            transpose_words(("w2", m, j, hf), halves(src[:, 2 * hf, :]) + halves(src[:, 2 * hf + 1, :]))

        def w2_regroup(engine, m, j, hf):
            if hf == 0:
                w2_g[(m, j)] = turn.tile([P, CHUNKS * K], BF16, name="w2_g%d" % m, align_bytes=64)
            regroup(engine, ("w2", m, j, hf), w2_g[(m, j)][:, 2 * K * hf : 2 * K * (hf + 1)])

        def w2_quantise(m, j):
            w2_q[(m, j)] = quantise(w2_g[(m, j)][:], "w2_%d" % m, turn)

        w3_g = {}
        w3_q = {}

        def w3_transpose(j):
            transpose_words(("w3", j), halves(w3_sb[0][j // 2][:, j % 2, :]) + halves(w3_sb[1][j // 2][:, j % 2, :]))

        def w3_regroup(j):
            w3_g[j] = turn.tile([P, 2 * K], BF16, name="w3_g", align_bytes=64)
            regroup("scalar", ("w3", j), w3_g[j][:])

        def w3_quantise(j):
            w3_q[j] = quantise(w3_g[j][:], "w3_%d" % j, keep)

        acc = {}
        hid = {}
        x2_q = {}

        def stage1(m, j):
            tag = "ls" if m == LS else "mu%d" % (j % 2)
            acc[(m, j)] = psum.tile([P, CHUNKS, P], F32, name="acc", tag=tag)
            for c in range(CHUNKS):
                pass_mx(
                    acc[(m, j)][:, c, :], w2_q[(m, j)], (x1_c, x1_s), slice(P * c, P * (c + 1)), slice(P * j, P * (j + 1))
                )

        def sigma_exp(j):
            hid[("e", j)] = turn.tile([P, CHUNKS, P], F32, name="e")
            for c in range(CHUNKS):
                nc.scalar.activation(
                    out=hid[("e", j)][:, c, :],
                    in_=acc[(LS, j)][:, c, :],
                    func=ACT.Exp,
                    bias=bias12[:, LS, j, c : c + 1],
                    scale=1.0,
                )

        def sigma_clip(j):
            hid[("sigma", j)] = turn.tile([P, CHUNKS, P], F32, name="sigma")
            nc.vector.tensor_scalar(
                out=hid[("sigma", j)][:],
                in0=hid[("e", j)][:],
                scalar1=clip_e[:, 0:1],
                scalar2=clip_e[:, 1:2],
                op0=ALU.max,
                op1=ALU.min,
            )

        def noise_and_sum(j):
            noisy = turn.tile([P, CHUNKS, P], F32, name="noisy")
            hid[("sum", j)] = turn.tile([P, CHUNKS, P], F32, name="total")
            for c in range(CHUNKS):
                nc.vector.scalar_tensor_tensor(
                    out=noisy[:, c, :],
                    in0=hid[("sigma", j)][:, c, :],
                    scalar=fac[:, 8 + CHUNKS * j + c : 9 + CHUNKS * j + c],
                    in1=row_fac[:, j, :],
                    op0=ALU.mult,
                    op1=ALU.mult,
                )
            for c in range(CHUNKS):
                nc.vector.scalar_tensor_tensor(
                    out=hid[("sum", j)][:, c, :],
                    in0=acc[(MU, j)][:, c, :],
                    scalar=bias12[:, MU, j, c : c + 1],
                    in1=noisy[:, c, :],
                    op0=ALU.add,
                    op1=ALU.add,
                )

        def relu_regroup(j):
            hid[("x2", j)] = turn.tile([P, K], BF16, name="x2_g", align_bytes=64)
            if j < RELU_ON_SCALAR_FROM:
                nc.vector.tensor_scalar_max(
                    out=hid[("x2", j)][:].rearrange("p (g i c) -> p g c i", i=4, c=CHUNKS),
                    in0=hid[("sum", j)][:].rearrange("p c (g i) -> p g c i", i=4),
                    scalar1=0.0,
                )
            else:
                nc.scalar.activation(
                    out=hid[("x2", j)][:].rearrange("p (b c) -> p b c", c=CHUNKS),
                    in_=hid[("sum", j)][:].rearrange("p c b -> p b c"),
                    func=ACT.Relu,
                )

        def x2_quantise(j):
            x2_q[j] = quantise(hid[("x2", j)][:], "x2_%d" % j, keep)

        def stage2(q):
            bank = next_bank(("heads", q))
            for i in range(2):
                j = 2 * q + i
                pass_mx(
                    bank[:, 2 * i : 2 * i + 2, :].rearrange("p m o -> p (m o)"),
                    x2_q[j],
                    w3_q[j],
                    slice(0, P),
                    slice(0, 2 * P),
                )

        def heads_out(q):
            sums = bank_of[("heads", q)][:].rearrange("p (i m) o -> p i m o", m=2)
            res = keep.tile([P, 2, 2, P], F32, name="res%d" % q)
            pair = slice(2 * q, 2 * q + 2)
            for m in (1, 0):
                nc.vector.tensor_tensor(out=res[:, :, m, :], in0=sums[:, :, m, :], in1=bias3[:, pair, m, :], op=ALU.add)
            nc.sync.dma_start(out=out_0[:, pair, :], in_=res[:, :, 0, :])
            nc.vector.tensor_scalar(
                out=res[:, :, 1, :], in0=res[:, :, 1, :], scalar1=-20.0, scalar2=2.0, op0=ALU.max, op1=ALU.min
            )
            nc.sync.dma_start(out=out_1[:, pair, :], in_=res[:, :, 1, :])

        def live(j):
            return 0 <= j < NM

        small_vectors()
        for q in range(NM // 2):
            x1_transpose(q)
            x1_regroup(q)
        x1_quantise(0)
        x1_quantise(1)
        for h in range(2):
            spread_row_factor(h)
            keep_row_factor(h)

        for j in range(-2, NM):
            if live(j + 1):
                w2_regroup("scalar", MU, j + 1, 0)
                w2_regroup("scalar", MU, j + 1, 1)
            if live(j):
                w3_transpose(j)
            if live(j + 2):
                w2_transpose(LS, j + 2, 0)
                w2_transpose(LS, j + 2, 1)
            if live(j):
                sigma_clip(j)
            if j == NM - 1:
                w3_quantise(j - 1)
            if live(j + 1):
                w2_quantise(LS, j + 1)
            if live(j):
                noise_and_sum(j)
                w3_regroup(j)
            if live(j + 2):
                w2_regroup("scalar", LS, j + 2, 0)
            if live(j + 1):
                stage1(LS, j + 1)
            if j in EARLY_HEADS:
                stage2(EARLY_HEADS[j])
            if live(j + 2):
                w2_transpose(MU, j + 2, 0)
                w2_transpose(MU, j + 2, 1)
            if live(j + 1):
                w2_quantise(MU, j + 1)
            if live(j) and j < RELU_ON_SCALAR_FROM:
                relu_regroup(j)
            if live(j + 2):
                w2_regroup("vector" if j < 0 else "scalar", LS, j + 2, 1)
            if j == -1:
                x1_quantise(2)
                x1_quantise(3)
            if live(j + 1):
                sigma_exp(j + 1)
            if live(j) and j >= RELU_ON_SCALAR_FROM:
                relu_regroup(j)
            if live(j) and j < NM - 2:
                w3_quantise(j)
                x2_quantise(j)
            if j in EARLY_HEADS:
                heads_out(EARLY_HEADS[j])
            if live(j + 1):
                stage1(MU, j + 1)

        late = [q for q in range(NM // 2) if q not in EARLY_HEADS.values()]
        for q in late[:-1]:
            stage2(q)
        x2_quantise(NM - 2)
        w3_quantise(NM - 1)
        for q in late[:1]:
            heads_out(q)
        x2_quantise(NM - 1)
        stage2(late[-1])
        for q in late[1:]:
            heads_out(q)
